import numpy as np
import ml_dtypes


def mxq(x, axis, fmt="e4m3"):
    dtype, down = {"e4m3": (ml_dtypes.float8_e4m3fn, 7), "e5m2": (ml_dtypes.float8_e5m2, 14)}[fmt]
    v = np.moveaxis(np.asarray(x, np.float32).astype(ml_dtypes.bfloat16).astype(np.float64), axis, -1)
    blocks = v.reshape(v.shape[:-1] + (-1, 32))
    amax = np.abs(blocks).max(-1, keepdims=True)
    byte = np.maximum(np.where(amax > 0, np.frexp(amax)[1] - 1 + 127, 0) - down, 1)
    scale = np.exp2(byte - 127.0)
    codes = (blocks / scale).astype(np.float32).astype(dtype).astype(np.float64)
    return np.moveaxis((codes * scale).reshape(v.shape), -1, axis)


WIDE = False


def mx_kscale(k):
    if not WIDE:
        return np.ones(k)
    levels = np.array([30, -30])
    if k % 512:
        return np.exp2(np.random.permutation(np.resize(levels, k // 32))).repeat(32)
    a = np.empty((k // 512, 16))
    for p in range(k // 512):
        a[p, :8] = np.random.permutation(np.resize(levels, 8))
        for g in range(8):
            far = levels[np.abs(levels - a[p, g]) >= 10]
            a[p, g + 8] = far[np.random.randint(len(far))]
    return np.exp2(a.ravel()).repeat(32)


BF16 = ml_dtypes.bfloat16


def bf(x):
    return np.asarray(x, np.float32).astype(BF16)


def f64(x):
    return np.asarray(x).astype(np.float64)


E2M1 = np.array([0.0, 0.5, 1.0, 1.5, 2.0, 3.0, 4.0, 6.0, -0.0, -0.5, -1.0, -1.5, -2.0, -3.0, -4.0, -6.0])


def pack_weight(w, fmt):
    k, n = w.shape
    w = f64(bf(w)).reshape(k // 32, 32, n)
    amax = np.abs(w).max(1)
    if fmt == "e4m3":
        byte = np.frexp(amax)[1] - 1 + 127 - 7
    else:
        mant, ex = np.frexp(amax / 6.0)
        byte = np.where(mant > 0.5, ex, ex - 1) + 127
    byte = np.clip(np.where(amax > 0, byte, 1), 1, 254)
    scaled = (w * np.exp2(127.0 - byte)[:, None, :]).reshape(k, n).astype(np.float32)
    by_word = np.ascontiguousarray(scaled.reshape(k // 512, 128, 4, n).transpose(0, 1, 3, 2))
    if fmt == "e4m3":
        words = by_word.astype(ml_dtypes.float8_e4m3fn).view(np.uint8)
    else:
        c = by_word.astype(ml_dtypes.float4_e2m1fn).view(np.uint8) & 0xF
        words = c[..., 0::2] | (c[..., 1::2] << 4)
    return np.ascontiguousarray(words), np.ascontiguousarray(byte.astype(np.uint8).reshape(k // 512, 16, n))


def unpack_weight(words, scales, fmt):
    g, p, n, _ = words.shape
    if fmt == "e4m3":
        vals = np.ascontiguousarray(words).view(ml_dtypes.float8_e4m3fn).astype(np.float64)
    else:
        nib = np.empty((g, p, n, 4), np.uint8)
        nib[..., 0::2] = words & 0xF
        nib[..., 1::2] = words >> 4
        vals = E2M1[nib]
    vals = vals * np.repeat(np.exp2(scales.astype(np.float64) - 127.0), 8, axis=1)[..., None]
    return vals.transpose(0, 1, 3, 2).reshape(g * 512, n)

def pack4(w):
    words, scales = pack_weight(w, "e2m1")
    return words.reshape(words.shape[0], 128, -1), scales


def unpack4(words, scales):
    return unpack_weight(words.reshape(words.shape[0], 128, -1, 2), scales, "e2m1")


B, S, D, H, HKV, HD, WINDOW, KB = 1, 512, 2048, 16, 8, 128, 256, 512
EPS = 1e-6
THETA = 10000.0


def rope_tables():
    inv_freq = 1.0 / THETA ** (np.arange(0, HD, 2) / HD)
    ang = np.arange(S)[:, None] * inv_freq[None, :]
    emb = np.concatenate([ang, ang], axis=-1)
    return np.broadcast_to(np.cos(emb)[None], (B, S, HD)), np.broadcast_to(np.sin(emb)[None], (B, S, HD))


def rms_norm(x, gain):
    var = np.mean(x * x, axis=-1, keepdims=True)
    return x * (1.0 / np.sqrt(var + EPS)) * gain


def rotate_half(x):
    return np.concatenate([-x[..., HD // 2:], x[..., :HD // 2]], axis=-1)


def apply_rope(x, cos, sin):
    return x * cos[:, :, None, :] + rotate_half(x) * sin[:, :, None, :]


def setup_inputs():
    s = mx_kscale(D)
    cos, sin = rope_tables()
    hidden_states = bf(np.random.standard_normal((B, S, D)) * s)
    Wq_words, Wq_scales = pack4(np.random.standard_normal((D, H * HD)) / np.sqrt(D) / s[:, None])
    Wk_words, Wk_scales = pack4(np.random.standard_normal((D, HKV * HD)) / np.sqrt(D) / s[:, None])
    Wv_words, Wv_scales = pack4(np.random.standard_normal((D, HKV * HD)) * 2.0 / np.sqrt(D) / s[:, None])
    q_scale = bf(np.random.uniform(0.5, 1.5, HD))
    k_scale = bf(np.random.uniform(0.5, 1.5, HD))
    return {
        "hidden_states": hidden_states,
        "cos": bf(cos),
        "sin": bf(sin),
        "Wq_words": Wq_words,
        "Wq_scales": Wq_scales,
        "Wk_words": Wk_words,
        "Wk_scales": Wk_scales,
        "Wv_words": Wv_words,
        "Wv_scales": Wv_scales,
        "q_scale": q_scale,
        "k_scale": k_scale,
    }


def reference(hidden_states, cos, sin, Wq_words, Wq_scales, Wk_words, Wk_scales, Wv_words, Wv_scales, q_scale, k_scale):
    xq = mxq(f64(hidden_states), 2, "e5m2")
    q = (xq @ unpack4(Wq_words, Wq_scales)).reshape(B, S, H, HD)
    k = (xq @ unpack4(Wk_words, Wk_scales)).reshape(B, S, HKV, HD)
    v = (xq @ unpack4(Wv_words, Wv_scales)).reshape(B, S, HKV, HD)
    q = rms_norm(q, f64(q_scale))
    k = rms_norm(k, f64(k_scale))
    q = apply_rope(q, f64(cos), f64(sin))
    k = apply_rope(k, f64(cos), f64(sin))
    return q, k, v

@@ -1,0 +1,241 @@
+from contextlib import ExitStack
+
+import concourse.mybir as mybir
+from concourse.masks import make_identity
+
+S, D, HD = 512, 2048, 128
+Q_COLS, KV_COLS = 2048, 1024
+EPS = 1e-6
+FLOPS = 2 * S * D * (Q_COLS + 2 * KV_COLS)
+
+F32 = mybir.dt.float32
+BF16 = mybir.dt.bfloat16
+I32 = mybir.dt.int32
+U32 = mybir.dt.uint32
+U8 = mybir.dt.uint8
+E5M2X4 = mybir.dt.float8_e5m2_x4
+E2M1X4 = mybir.dt.float4_e2m1fn_x4
+ACT = mybir.ActivationFunctionType
+ALU = mybir.AluOpType
+
+P = 128
+TOKEN_TILES = S // P
+PASSES = D // 512
+BANK = 512
+BANKS = 8
+HEADS = BANK // HD
+HALF = HD // 2
+
+
+def tile_multiheadattention_pa_kernel(
+    tc, hidden_states, cos, sin, Wq_words, Wq_scales, Wk_words, Wk_scales, Wv_words, Wv_scales,
+    q_scale, k_scale, out_0, out_1, out_2,
+):
+    nc = tc.nc
+    x_rows = hidden_states[0].rearrange("(p t) k -> p t k", t=TOKEN_TILES)
+    outs = {
+        "q": out_0[0].rearrange("(p t) h d -> p t (h d)", t=TOKEN_TILES),
+        "k": out_1[0].rearrange("(p t) h d -> p t (h d)", t=TOKEN_TILES),
+        "v": out_2[0].rearrange("(p t) h d -> p t (h d)", t=TOKEN_TILES),
+    }
+    words_hbm = {"q": Wq_words, "k": Wk_words, "v": Wv_words}
+    scales_hbm = {"q": Wq_scales, "k": Wk_scales, "v": Wv_scales}
+
+    with ExitStack() as ctx:
+        keep = ctx.enter_context(tc.tile_pool(name="keep", bufs=1))
+        work = ctx.enter_context(tc.tile_pool(name="work", bufs=4))
+        results = ctx.enter_context(tc.tile_pool(name="results", bufs=16))
+        psum = ctx.enter_context(tc.psum_pool(name="psum", bufs=1))
+        ctx.enter_context(tc.manual_schedule())
+
+        def bank(number):
+            return psum.tile([P, BANK], F32, name="bank%d" % number)
+
+        identity = keep.tile([P, P], F32)
+        make_identity(nc, identity[:])
+
+        gain_rows = keep.tile([P, 2 * HD], BF16)
+        ones = keep.tile([P, P], BF16)
+        nc.vector.memset(gain_rows[:], 0.0)
+        nc.vector.memset(ones[:], 1.0)
+        nc.scalar.dma_start(out=gain_rows[0:1, 0:HD], in_=q_scale.unsqueeze(0))
+        nc.scalar.dma_start(out=gain_rows[0:1, HD : 2 * HD], in_=k_scale.unsqueeze(0))
+
+        spans = [("q", 0, 1), ("q", 1, 1), ("q", 2, 2), ("k", 0, 2), ("v", 0, 2)]
+        planes = {}
+        for name, first, count in spans:
+            plane = keep.tile([P, PASSES, count * BANK], U8, name="plane_%s%d" % (name, first), align_bytes=64)
+            nc.vector.memset(plane[:].bitcast(I32), 0)
+            for c in range(count):
+                planes[(name, first + c)] = (plane, c)
+
+        def load_scales(name, first, count):
+            plane = planes[(name, first)][0]
+            for r in range(4):
+                rows = scales_hbm[name][:, r:16:4, first * BANK : (first + count) * BANK]
+                nc.sync.dma_start(
+                    out=plane[r:P:32, :, :].bitcast(I32), in_=rows.rearrange("g q n -> q g n").bitcast(I32)
+                )
+
+        words = {}
+
+        def load_words(name, first, count):
+            tile = keep.tile([P, PASSES, count * 2 * BANK], U8, name="words_%s%d" % (name, first), align_bytes=64)
+            src = words_hbm[name][:, :, first * 2 * BANK : (first + count) * 2 * BANK]
+            nc.sync.dma_start(out=tile[:].bitcast(I32), in_=src.rearrange("g p n -> p g n").bitcast(I32))
+            for c in range(count):
+                words[(name, first + c)] = (tile, c)
+
+        x_sb = {}
+
+        def load_x(t, pieces):
+            width = D // pieces
+            for piece in range(pieces):
+                tile = keep.tile([P, width], BF16, name="x%d_%d" % (t, piece))
+                nc.sync.dma_start(out=tile[:], in_=x_rows[:, t, piece * width : (piece + 1) * width])
+                for g in range(PASSES // pieces):
+                    x_sb[(t, piece * (PASSES // pieces) + g)] = tile[:].bitcast(F32)[:, g * 256 : (g + 1) * 256]
+
+        cos_sb = keep.tile([P, TOKEN_TILES, 2, HALF], BF16)
+        sin_sb = keep.tile([P, TOKEN_TILES, 2, HALF], BF16)
+
+        load_x(0, 2)
+        load_x(1, 1)
+        load_scales(*spans[0])
+        load_words(*spans[0])
+        load_x(2, 1)
+        nc.sync.dma_start(out=cos_sb[:], in_=cos[0].rearrange("(p t) (u d) -> p t u d", t=TOKEN_TILES, u=2))
+        nc.sync.dma_start(out=sin_sb[:], in_=sin[0].rearrange("(p t) (u d) -> p t u d", t=TOKEN_TILES, u=2))
+        load_scales(*spans[1])
+        load_words(*spans[1])
+        load_x(3, 1)
+        for span in spans[2:]:
+            load_scales(*span)
+        for span in spans[2:]:
+            load_words(*span)
+
+        turned = {}
+        codes = {}
+
+        def transpose_tokens(t):
+            for half in range(2):
+                xt = bank(2 * (t % 2) + half)
+                for g in range(2):
+                    pass_words = x_sb[(t, 2 * half + g)]
+                    for u in range(2):
+                        at = (2 * g + u) * P
+                        nc.tensor.transpose(xt[:, at : at + P], pass_words[:, u:256:2], identity[:])
+                turned[(t, half)] = xt
+
+        def quantize_tokens(t):
+            for half in range(2):
+                grouped = work.tile([P, 2 * P * 4], BF16, align_bytes=64)
+                nc.scalar.copy(
+                    out=grouped[:].bitcast(F32).rearrange("p (g r u) -> p g r u", g=2, u=2),
+                    in_=turned[(t, half)][:].rearrange("p (g u r) -> p g r u", g=2, u=2),
+                )
+                x_codes = keep.tile([P, 2 * P], U32, name="codes%d_%d" % (t, half), align_bytes=64)
+                x_plane = keep.tile([P, 2 * P], U8, name="xplane%d_%d" % (t, half), align_bytes=64)
+                nc.vector.quantize_mx(out=x_codes[:].bitcast(E5M2X4), scales=x_plane[:], in_=grouped[:])
+                for g in range(2):
+                    codes[(t, 2 * half + g)] = (x_codes[:, g * P : (g + 1) * P], x_plane[:, g * P : (g + 1) * P])
+
+        tables = {}
+
+        def build_tables():
+            spread = bank(BANKS - 1)
+            nc.tensor.matmul(spread[:, 0 : 2 * HD], lhsT=ones[:], rhs=gain_rows[:], start=True, stop=True)
+            for w, name in enumerate("qk"):
+                gain = spread[:, w * HD : (w + 1) * HD].rearrange("p (u d) -> p u d", u=2)
+                table = keep.tile([P, TOKEN_TILES, 4, HALF], F32, name="table_" + name)
+                nc.vector.tensor_tensor(
+                    out=table[:, :, 0:4:3, :], in0=cos_sb[:],
+                    in1=gain.unsqueeze(1).to_broadcast([P, TOKEN_TILES, 2, HALF]), op=ALU.mult,
+                )
+                nc.vector.scalar_tensor_tensor(
+                    out=table[:, :, 1, :], in0=sin_sb[:, :, 0, :], scalar=-1.0,
+                    in1=gain[:, 1:2, :].to_broadcast([P, TOKEN_TILES, HALF]), op0=ALU.mult, op1=ALU.mult,
+                )
+                nc.vector.tensor_tensor(
+                    out=table[:, :, 2, :], in0=sin_sb[:, :, 1, :],
+                    in1=gain[:, 0:1, :].to_broadcast([P, TOKEN_TILES, HALF]), op=ALU.mult,
+                )
+                tables[name] = table
+
+        def project(number, name, c, t, first=0, width=BANK):
+            acc = bank((4 + number) % BANKS)
+            tile, at = words[(name, c)]
+            plane = planes[(name, c)][0]
+            col = at * BANK + first
+            for g in range(PASSES):
+                x_codes, x_plane = codes[(t, g)]
+                nc.tensor.matmul_mx(
+                    out=acc[:, 0:width],
+                    lhsT=x_codes.bitcast(E5M2X4),
+                    lhsT_scale=x_plane,
+                    rhs=tile[:, g, 2 * col : 2 * (col + width)].bitcast(E2M1X4),
+                    rhs_scale=plane[:, g, col : col + width],
+                    start=(g == 0),
+                    stop=(g == PASSES - 1),
+                )
+            return acc
+
+        def finish(acc, name, c, t, adder):
+            result = results.tile([P, BANK], F32)
+            if name == "v":
+                nc.scalar.copy(out=result[:], in_=acc[:])
+            else:
+                squares = work.tile([P, BANK], BF16)
+                sums = work.tile([P, HEADS], F32)
+                rstd = work.tile([P, HEADS], F32)
+                for h in range(HEADS):
+                    cols = slice(h * HD, (h + 1) * HD)
+                    nc.scalar.activation(
+                        out=squares[:, cols], in_=acc[:, cols], func=ACT.Square, accum_out=sums[:, h : h + 1]
+                    )
+                nc.scalar.activation(
+                    out=rstd[:], in_=sums[:], func=ACT.Abs_reciprocal_sqrt, scale=1.0 / HD, bias=EPS
+                )
+                products = work.tile([P, HEADS, 2, HD], F32, bufs=8)
+                table = tables[name][:, t, :, :].rearrange("p (j u) d -> p j (u d)", j=2)
+                for h in range(HEADS):
+                    nc.vector.scalar_tensor_tensor(
+                        out=products[:, h, :, :],
+                        in0=acc[:, h * HD : (h + 1) * HD].unsqueeze(1).to_broadcast([P, 2, HD]),
+                        scalar=rstd[:, h : h + 1], in1=table, op0=ALU.mult, op1=ALU.mult,
+                    )
+                terms = products[:].rearrange("p h j (u d) -> p (h j) u d", u=2)
+                adder.tensor_tensor(
+                    out=result[:].rearrange("p (m d) -> p m d", d=HALF),
+                    in0=terms[:, :, 0, :], in1=terms[:, :, 1, :], op=ALU.add,
+                )
+            queue = nc.scalar if name == "v" else nc.sync
+            queue.dma_start(out=outs[name][:, t, c * BANK : (c + 1) * BANK], in_=result[:])
+
+        tokens = range(TOKEN_TILES)
+        groups = [("q", c, t) for c in (0, 1) for t in (0, 1)]
+        groups += [("q", c, t) for t in (2, 3) for c in (0, 1)]
+        groups += [g + (t,) for t in tokens for g in (("q", 2), ("q", 3), ("k", 0), ("k", 1), ("v", 0))]
+        groups += [("v", 1, t) for t in tokens]
+        late_tokens = {0: 2, 2: 3}
+
+        for t in (0, 1):
+            transpose_tokens(t)
+            quantize_tokens(t)
+        build_tables()
+        for number, (name, c, t) in enumerate(groups[:-1]):
+            acc = project(number, name, c, t)
+            if number in late_tokens:
+                transpose_tokens(late_tokens[number])
+            finish(acc, name, c, t, nc.vector if (name, t) == ("k", TOKEN_TILES - 1) else nc.gpsimd)
+            if number in late_tokens:
+                quantize_tokens(late_tokens[number])
+
+        name, c, t = groups[-1]
+        width = BANK // 2
+        for piece, copy in enumerate((nc.vector.tensor_copy, nc.scalar.copy)):
+            acc = project(len(groups) - 1 + piece, name, c, t, piece * width, width)
+            last = results.tile([P, width], F32)
+            copy(out=last[:], in_=acc[:, 0:width])
+            col = c * BANK + piece * width
+            (nc.sync, nc.scalar)[piece].dma_start(out=outs[name][:, t, col : col + width], in_=last[:])

@@ -44,7 +44,7 @@ def tile_multiheadattention_pa_kernel(
     with ExitStack() as ctx:
         keep = ctx.enter_context(tc.tile_pool(name="keep", bufs=1))
         work = ctx.enter_context(tc.tile_pool(name="work", bufs=4))
-        results = ctx.enter_context(tc.tile_pool(name="results", bufs=16))
+        results = ctx.enter_context(tc.tile_pool(name="results", bufs=8))
         psum = ctx.enter_context(tc.psum_pool(name="psum", bufs=1))
         ctx.enter_context(tc.manual_schedule())
 
@@ -60,6 +60,16 @@ def tile_multiheadattention_pa_kernel(
         nc.vector.memset(ones[:], 1.0)
         nc.scalar.dma_start(out=gain_rows[0:1, 0:HD], in_=q_scale.unsqueeze(0))
         nc.scalar.dma_start(out=gain_rows[0:1, HD : 2 * HD], in_=k_scale.unsqueeze(0))
+
+        filler = keep.tile([P, BANK], BF16)
+        nc.vector.memset(filler[:], 1.0)
+        primed = keep.tile([P, 1], F32)
+        nc.scalar.activation(out=primed[:], in_=ones[:, 0:1], func=ACT.Abs_reciprocal_sqrt)
+
+        def warm_up(count):
+            unused = bank(BANKS - 2)
+            for repeat in range(count):
+                nc.tensor.matmul(unused[:], lhsT=ones[:], rhs=filler[:], start=True, stop=True)
 
         spans = [("q", 0, 1), ("q", 1, 1), ("q", 2, 2), ("k", 0, 2), ("v", 0, 2)]
         planes = {}
@@ -103,15 +113,12 @@ def tile_multiheadattention_pa_kernel(
         load_x(1, 1)
         load_scales(*spans[0])
         load_words(*spans[0])
-        load_x(2, 1)
         nc.sync.dma_start(out=cos_sb[:], in_=cos[0].rearrange("(p t) (u d) -> p t u d", t=TOKEN_TILES, u=2))
         nc.sync.dma_start(out=sin_sb[:], in_=sin[0].rearrange("(p t) (u d) -> p t u d", t=TOKEN_TILES, u=2))
-        load_scales(*spans[1])
-        load_words(*spans[1])
+        load_x(2, 1)
         load_x(3, 1)
-        for span in spans[2:]:
+        for span in spans[1:]:
             load_scales(*span)
-        for span in spans[2:]:
             load_words(*span)
 
         turned = {}
@@ -162,12 +169,11 @@ def tile_multiheadattention_pa_kernel(
                 )
                 tables[name] = table
 
-        def project(number, name, c, t, first=0, width=BANK):
-            acc = bank((4 + number) % BANKS)
+        def project(acc, name, c, t, passes, first=0, width=BANK):
             tile, at = words[(name, c)]
             plane = planes[(name, c)][0]
             col = at * BANK + first
-            for g in range(PASSES):
+            for g in passes:
                 x_codes, x_plane = codes[(t, g)]
                 nc.tensor.matmul_mx(
                     out=acc[:, 0:width],
@@ -178,63 +184,96 @@ def tile_multiheadattention_pa_kernel(
                     start=(g == 0),
                     stop=(g == PASSES - 1),
                 )
-            return acc
 
-        def finish(acc, name, c, t, adder):
-            result = results.tile([P, BANK], F32)
-            if name == "v":
-                nc.scalar.copy(out=result[:], in_=acc[:])
-            else:
-                squares = work.tile([P, BANK], BF16)
-                sums = work.tile([P, HEADS], F32)
-                rstd = work.tile([P, HEADS], F32)
-                for h in range(HEADS):
-                    cols = slice(h * HD, (h + 1) * HD)
-                    nc.scalar.activation(
-                        out=squares[:, cols], in_=acc[:, cols], func=ACT.Square, accum_out=sums[:, h : h + 1]
-                    )
+        pair_products = {}
+
+        def sum_squares(acc, after_first):
+            squares = work.tile([P, BANK], BF16)
+            sums = work.tile([P, HEADS], F32)
+            for h in range(HEADS):
+                cols = slice(h * HD, (h + 1) * HD)
                 nc.scalar.activation(
-                    out=rstd[:], in_=sums[:], func=ACT.Abs_reciprocal_sqrt, scale=1.0 / HD, bias=EPS
+                    out=squares[:, cols], in_=acc[:, cols], func=ACT.Square, accum_out=sums[:, h : h + 1]
                 )
-                products = work.tile([P, HEADS, 2, HD], F32, bufs=8)
-                table = tables[name][:, t, :, :].rearrange("p (j u) d -> p j (u d)", j=2)
-                for h in range(HEADS):
-                    nc.vector.scalar_tensor_tensor(
-                        out=products[:, h, :, :],
-                        in0=acc[:, h * HD : (h + 1) * HD].unsqueeze(1).to_broadcast([P, 2, HD]),
-                        scalar=rstd[:, h : h + 1], in1=table, op0=ALU.mult, op1=ALU.mult,
-                    )
-                terms = products[:].rearrange("p h j (u d) -> p (h j) u d", u=2)
-                adder.tensor_tensor(
-                    out=result[:].rearrange("p (m d) -> p m d", d=HALF),
-                    in0=terms[:, :, 0, :], in1=terms[:, :, 1, :], op=ALU.add,
+                if h == 0:
+                    after_first()
+            return sums
+
+        def norm_factors(sums):
+            rstd = work.tile([P, HEADS], F32)
+            nc.scalar.activation(out=rstd[:], in_=sums[:], func=ACT.Abs_reciprocal_sqrt, scale=1.0 / HD, bias=EPS)
+            return rstd
+
+        def multiply(acc, rstd, name, c, t, heads):
+            if (name, c, t // 2) not in pair_products:
+                pair_products[(name, c, t // 2)] = work.tile([P, 2, HEADS, 2, HD], F32, name="products", bufs=6)
+            products = pair_products[(name, c, t // 2)]
+            table = tables[name][:, t, :, :].rearrange("p (j u) d -> p j (u d)", j=2)
+            for h in heads:
+                nc.vector.scalar_tensor_tensor(
+                    out=products[:, t % 2, h, :, :],
+                    in0=acc[:, h * HD : (h + 1) * HD].unsqueeze(1).to_broadcast([P, 2, HD]),
+                    scalar=rstd[:, h : h + 1], in1=table, op0=ALU.mult, op1=ALU.mult,
                 )
-            queue = nc.scalar if name == "v" else nc.sync
-            queue.dma_start(out=outs[name][:, t, c * BANK : (c + 1) * BANK], in_=result[:])
 
-        tokens = range(TOKEN_TILES)
-        groups = [("q", c, t) for c in (0, 1) for t in (0, 1)]
-        groups += [("q", c, t) for t in (2, 3) for c in (0, 1)]
-        groups += [g + (t,) for t in tokens for g in (("q", 2), ("q", 3), ("k", 0), ("k", 1), ("v", 0))]
-        groups += [("v", 1, t) for t in tokens]
-        late_tokens = {0: 2, 2: 3}
+        def add_and_store(name, c, t):
+            last = (name, c, t) == ("k", 1, TOKEN_TILES - 1)
+            terms = pair_products[(name, c, t // 2)][:].rearrange("p t h j (u d) -> p (t h j) u d", u=2)
+            rotated = results.tile([P, 2, BANK], F32)
+            (nc.vector if last else nc.gpsimd).tensor_tensor(
+                out=rotated[:].rearrange("p t (m d) -> p (t m) d", d=HALF),
+                in0=terms[:, :, 0, :], in1=terms[:, :, 1, :], op=ALU.add,
+            )
+            nc.sync.dma_start(out=outs[name][:, t - 1 : t + 1, c * BANK : (c + 1) * BANK], in_=rotated[:])
 
+        waiting = []
+
+        def rotate_waiting():
+            for acc, sums, name, c, t in waiting:
+                multiply(acc, norm_factors(sums), name, c, t, range(HEADS))
+                if t % 2 == 1:
+                    add_and_store(name, c, t)
+            waiting.clear()
+
+        columns = [("q", 0), ("q", 1), ("q", 2), ("q", 3), ("k", 0), ("k", 1), ("v", 0), ("v", 1)]
+        groups = [(name, c, t) for name, c in columns for t in range(TOKEN_TILES)]
+
+        warm_up(4)
         for t in (0, 1):
             transpose_tokens(t)
+            warm_up(2)
             quantize_tokens(t)
         build_tables()
         for number, (name, c, t) in enumerate(groups[:-1]):
-            acc = project(number, name, c, t)
-            if number in late_tokens:
-                transpose_tokens(late_tokens[number])
-            finish(acc, name, c, t, nc.vector if (name, t) == ("k", TOKEN_TILES - 1) else nc.gpsimd)
-            if number in late_tokens:
-                quantize_tokens(late_tokens[number])
+            acc = bank((4 + number) % BANKS)
+            if number == 1:
+                rotate_waiting()
+                project(acc, name, c, t, range(0, PASSES // 2))
+                transpose_tokens(2)
+                quantize_tokens(2)
+                project(acc, name, c, t, range(PASSES // 2, PASSES))
+                transpose_tokens(3)
+                rstd = norm_factors(sum_squares(acc, rotate_waiting))
+                multiply(acc, rstd, name, c, t, range(0, HEADS // 2))
+                quantize_tokens(3)
+                multiply(acc, rstd, name, c, t, range(HEADS // 2, HEADS))
+                add_and_store(name, c, t)
+                continue
+            project(acc, name, c, t, range(PASSES))
+            if name == "v":
+                value = results.tile([P, BANK], F32)
+                nc.scalar.copy(out=value[:], in_=acc[:])
+                rotate_waiting()
+                nc.scalar.dma_start(out=outs[name][:, t, c * BANK : (c + 1) * BANK], in_=value[:])
+                continue
+            sums = sum_squares(acc, rotate_waiting)
+            waiting.append((acc, sums, name, c, t))
 
         name, c, t = groups[-1]
         width = BANK // 2
         for piece, copy in enumerate((nc.vector.tensor_copy, nc.scalar.copy)):
-            acc = project(len(groups) - 1 + piece, name, c, t, piece * width, width)
+            acc = bank((4 + len(groups) - 1 + piece) % BANKS)
+            project(acc, name, c, t, range(PASSES), piece * width, width)
             last = results.tile([P, width], F32)
             copy(out=last[:], in_=acc[:, 0:width])
             col = c * BANK + piece * width

from contextlib import ExitStack

import concourse.mybir as mybir
from concourse.masks import make_identity

S, D, HD = 512, 2048, 128
Q_COLS, KV_COLS = 2048, 1024
EPS = 1e-6
FLOPS = 2 * S * D * (Q_COLS + 2 * KV_COLS)

F32 = mybir.dt.float32
BF16 = mybir.dt.bfloat16
I32 = mybir.dt.int32
U32 = mybir.dt.uint32
U8 = mybir.dt.uint8
E5M2X4 = mybir.dt.float8_e5m2_x4
E2M1X4 = mybir.dt.float4_e2m1fn_x4
ACT = mybir.ActivationFunctionType
ALU = mybir.AluOpType

P = 128
TOKEN_TILES = S // P
PASSES = D // 512
BANK = 512
BANKS = 8
HEADS = BANK // HD
HALF = HD // 2


def tile_multiheadattention_pa_kernel(
    tc, hidden_states, cos, sin, Wq_words, Wq_scales, Wk_words, Wk_scales, Wv_words, Wv_scales,
    q_scale, k_scale, out_0, out_1, out_2,
):
    nc = tc.nc
    x_rows = hidden_states[0].rearrange("(p t) k -> p t k", t=TOKEN_TILES)
    outs = {
        "q": out_0[0].rearrange("(p t) h d -> p t (h d)", t=TOKEN_TILES),
        "k": out_1[0].rearrange("(p t) h d -> p t (h d)", t=TOKEN_TILES),
        "v": out_2[0].rearrange("(p t) h d -> p t (h d)", t=TOKEN_TILES),
    }
    words_hbm = {"q": Wq_words, "k": Wk_words, "v": Wv_words}
    scales_hbm = {"q": Wq_scales, "k": Wk_scales, "v": Wv_scales}

    with ExitStack() as ctx:
        keep = ctx.enter_context(tc.tile_pool(name="keep", bufs=1))
        work = ctx.enter_context(tc.tile_pool(name="work", bufs=4))
        results = ctx.enter_context(tc.tile_pool(name="results", bufs=8))
        psum = ctx.enter_context(tc.psum_pool(name="psum", bufs=1))
        ctx.enter_context(tc.manual_schedule())

        def bank(number):
            return psum.tile([P, BANK], F32, name="bank%d" % number)

        identity = keep.tile([P, P], F32)
        make_identity(nc, identity[:])

        gain_rows = keep.tile([P, 2 * HD], BF16)
        ones = keep.tile([P, P], BF16)
        nc.vector.memset(gain_rows[:], 0.0)
        nc.vector.memset(ones[:], 1.0)
        nc.scalar.dma_start(out=gain_rows[0:1, 0:HD], in_=q_scale.unsqueeze(0))
        nc.scalar.dma_start(out=gain_rows[0:1, HD : 2 * HD], in_=k_scale.unsqueeze(0))

        filler = keep.tile([P, BANK], BF16)
        nc.vector.memset(filler[:], 1.0)
        primed = keep.tile([P, 1], F32)
        nc.scalar.activation(out=primed[:], in_=ones[:, 0:1], func=ACT.Abs_reciprocal_sqrt)

        def warm_up(count):
            unused = bank(BANKS - 2)
            for repeat in range(count):
                nc.tensor.matmul(unused[:], lhsT=ones[:], rhs=filler[:], start=True, stop=True)

        spans = [("q", 0, 1), ("q", 1, 1), ("q", 2, 2), ("k", 0, 2), ("v", 0, 2)]
        planes = {}
        for name, first, count in spans:
            plane = keep.tile([P, PASSES, count * BANK], U8, name="plane_%s%d" % (name, first), align_bytes=64)
            nc.vector.memset(plane[:].bitcast(I32), 0)
            for c in range(count):
                planes[(name, first + c)] = (plane, c)

        def load_scales(name, first, count):
            plane = planes[(name, first)][0]
            for r in range(4):
                rows = scales_hbm[name][:, r:16:4, first * BANK : (first + count) * BANK]
                nc.sync.dma_start(
                    out=plane[r:P:32, :, :].bitcast(I32), in_=rows.rearrange("g q n -> q g n").bitcast(I32)
                )

        words = {}

        def load_words(name, first, count):
            tile = keep.tile([P, PASSES, count * 2 * BANK], U8, name="words_%s%d" % (name, first), align_bytes=64)
            src = words_hbm[name][:, :, first * 2 * BANK : (first + count) * 2 * BANK]
            nc.sync.dma_start(out=tile[:].bitcast(I32), in_=src.rearrange("g p n -> p g n").bitcast(I32))
            for c in range(count):
                words[(name, first + c)] = (tile, c)

        x_sb = {}

        def load_x(t, pieces):
            width = D // pieces
            for piece in range(pieces):
                tile = keep.tile([P, width], BF16, name="x%d_%d" % (t, piece))
                nc.sync.dma_start(out=tile[:], in_=x_rows[:, t, piece * width : (piece + 1) * width])
                for g in range(PASSES // pieces):
                    x_sb[(t, piece * (PASSES // pieces) + g)] = tile[:].bitcast(F32)[:, g * 256 : (g + 1) * 256]

        cos_sb = keep.tile([P, TOKEN_TILES, 2, HALF], BF16)
        sin_sb = keep.tile([P, TOKEN_TILES, 2, HALF], BF16)

        load_x(0, 2)
        load_x(1, 1)
        load_scales(*spans[0])
        load_words(*spans[0])
        nc.sync.dma_start(out=cos_sb[:], in_=cos[0].rearrange("(p t) (u d) -> p t u d", t=TOKEN_TILES, u=2))
        nc.sync.dma_start(out=sin_sb[:], in_=sin[0].rearrange("(p t) (u d) -> p t u d", t=TOKEN_TILES, u=2))
        load_x(2, 1)
        load_x(3, 1)
        for span in spans[1:]:
            load_scales(*span)
            load_words(*span)

        turned = {}
        codes = {}

        def transpose_tokens(t):
            for half in range(2):
                xt = bank(2 * (t % 2) + half)
                for g in range(2):
                    pass_words = x_sb[(t, 2 * half + g)]
                    for u in range(2):
                        at = (2 * g + u) * P
                        nc.tensor.transpose(xt[:, at : at + P], pass_words[:, u:256:2], identity[:])
                turned[(t, half)] = xt

        def quantize_tokens(t):
            for half in range(2):
                grouped = work.tile([P, 2 * P * 4], BF16, align_bytes=64)
                nc.scalar.copy(
                    out=grouped[:].bitcast(F32).rearrange("p (g r u) -> p g r u", g=2, u=2),
                    in_=turned[(t, half)][:].rearrange("p (g u r) -> p g r u", g=2, u=2),
                )
                x_codes = keep.tile([P, 2 * P], U32, name="codes%d_%d" % (t, half), align_bytes=64)
                x_plane = keep.tile([P, 2 * P], U8, name="xplane%d_%d" % (t, half), align_bytes=64)
                nc.vector.quantize_mx(out=x_codes[:].bitcast(E5M2X4), scales=x_plane[:], in_=grouped[:])
                for g in range(2):
                    codes[(t, 2 * half + g)] = (x_codes[:, g * P : (g + 1) * P], x_plane[:, g * P : (g + 1) * P])

        tables = {}

        def build_tables():
            spread = bank(BANKS - 1)
            nc.tensor.matmul(spread[:, 0 : 2 * HD], lhsT=ones[:], rhs=gain_rows[:], start=True, stop=True)
            for w, name in enumerate("qk"):
                gain = spread[:, w * HD : (w + 1) * HD].rearrange("p (u d) -> p u d", u=2)
                table = keep.tile([P, TOKEN_TILES, 4, HALF], F32, name="table_" + name)
                nc.vector.tensor_tensor(
                    out=table[:, :, 0:4:3, :], in0=cos_sb[:],
                    in1=gain.unsqueeze(1).to_broadcast([P, TOKEN_TILES, 2, HALF]), op=ALU.mult,
                )
                nc.vector.scalar_tensor_tensor(
                    out=table[:, :, 1, :], in0=sin_sb[:, :, 0, :], scalar=-1.0,
                    in1=gain[:, 1:2, :].to_broadcast([P, TOKEN_TILES, HALF]), op0=ALU.mult, op1=ALU.mult,
                )
                nc.vector.tensor_tensor(
                    out=table[:, :, 2, :], in0=sin_sb[:, :, 1, :],
                    in1=gain[:, 0:1, :].to_broadcast([P, TOKEN_TILES, HALF]), op=ALU.mult,
                )
                tables[name] = table

        def project(acc, name, c, t, passes, first=0, width=BANK):
            tile, at = words[(name, c)]
            plane = planes[(name, c)][0]
            col = at * BANK + first
            for g in passes:
                x_codes, x_plane = codes[(t, g)]
                nc.tensor.matmul_mx(
                    out=acc[:, 0:width],
                    lhsT=x_codes.bitcast(E5M2X4),
                    lhsT_scale=x_plane,
                    rhs=tile[:, g, 2 * col : 2 * (col + width)].bitcast(E2M1X4),
                    rhs_scale=plane[:, g, col : col + width],
                    start=(g == 0),
                    stop=(g == PASSES - 1),
                )

        pair_products = {}

        def sum_squares(acc, after_first):
            squares = work.tile([P, BANK], BF16)
            sums = work.tile([P, HEADS], F32)
            for h in range(HEADS):
                cols = slice(h * HD, (h + 1) * HD)
                nc.scalar.activation(
                    out=squares[:, cols], in_=acc[:, cols], func=ACT.Square, accum_out=sums[:, h : h + 1]
                )
                if h == 0:
                    after_first()
            return sums

        def norm_factors(sums):
            rstd = work.tile([P, HEADS], F32)
            nc.scalar.activation(out=rstd[:], in_=sums[:], func=ACT.Abs_reciprocal_sqrt, scale=1.0 / HD, bias=EPS)
            return rstd

        def multiply(acc, rstd, name, c, t, heads):
            if (name, c, t // 2) not in pair_products:
                pair_products[(name, c, t // 2)] = work.tile([P, 2, HEADS, 2, HD], F32, name="products", bufs=6)
            products = pair_products[(name, c, t // 2)]
            table = tables[name][:, t, :, :].rearrange("p (j u) d -> p j (u d)", j=2)
            for h in heads:
                nc.vector.scalar_tensor_tensor(
                    out=products[:, t % 2, h, :, :],
                    in0=acc[:, h * HD : (h + 1) * HD].unsqueeze(1).to_broadcast([P, 2, HD]),
                    scalar=rstd[:, h : h + 1], in1=table, op0=ALU.mult, op1=ALU.mult,
                )

        def add_and_store(name, c, t):
            last = (name, c, t) == ("k", 1, TOKEN_TILES - 1)
            terms = pair_products[(name, c, t // 2)][:].rearrange("p t h j (u d) -> p (t h j) u d", u=2)
            rotated = results.tile([P, 2, BANK], F32)
            (nc.vector if last else nc.gpsimd).tensor_tensor(
                out=rotated[:].rearrange("p t (m d) -> p (t m) d", d=HALF),
                in0=terms[:, :, 0, :], in1=terms[:, :, 1, :], op=ALU.add,
            )
            nc.sync.dma_start(out=outs[name][:, t - 1 : t + 1, c * BANK : (c + 1) * BANK], in_=rotated[:])

        waiting = []

        def rotate_waiting():
            for acc, sums, name, c, t in waiting:
                multiply(acc, norm_factors(sums), name, c, t, range(HEADS))
                if t % 2 == 1:
                    add_and_store(name, c, t)
            waiting.clear()

        columns = [("q", 0), ("q", 1), ("q", 2), ("q", 3), ("k", 0), ("k", 1), ("v", 0), ("v", 1)]
        groups = [(name, c, t) for name, c in columns for t in range(TOKEN_TILES)]

        warm_up(4)
        for t in (0, 1):
            transpose_tokens(t)
            warm_up(2)
            quantize_tokens(t)
        build_tables()
        for number, (name, c, t) in enumerate(groups[:-1]):
            acc = bank((4 + number) % BANKS)
            if number == 1:
                rotate_waiting()
                project(acc, name, c, t, range(0, PASSES // 2))
                transpose_tokens(2)
                quantize_tokens(2)
                project(acc, name, c, t, range(PASSES // 2, PASSES))
                transpose_tokens(3)
                rstd = norm_factors(sum_squares(acc, rotate_waiting))
                multiply(acc, rstd, name, c, t, range(0, HEADS // 2))
                quantize_tokens(3)
                multiply(acc, rstd, name, c, t, range(HEADS // 2, HEADS))
                add_and_store(name, c, t)
                continue
            project(acc, name, c, t, range(PASSES))
            if name == "v":
                value = results.tile([P, BANK], F32)
                nc.scalar.copy(out=value[:], in_=acc[:])
                rotate_waiting()
                nc.scalar.dma_start(out=outs[name][:, t, c * BANK : (c + 1) * BANK], in_=value[:])
                continue
            sums = sum_squares(acc, rotate_waiting)
            waiting.append((acc, sums, name, c, t))

        name, c, t = groups[-1]
        width = BANK // 2
        for piece, copy in enumerate((nc.vector.tensor_copy, nc.scalar.copy)):
            acc = bank((4 + len(groups) - 1 + piece) % BANKS)
            project(acc, name, c, t, range(PASSES), piece * width, width)
            last = results.tile([P, width], F32)
            copy(out=last[:], in_=acc[:, 0:width])
            col = c * BANK + piece * width
            (nc.sync, nc.scalar)[piece].dma_start(out=outs[name][:, t, col : col + width], in_=last[:])
